import numpy as np
import ml_dtypes


def mxq(x, axis, fmt="e4m3"):
    dtype, down = {"e4m3": (ml_dtypes.float8_e4m3fn, 7), "e5m2": (ml_dtypes.float8_e5m2, 14)}[fmt]
    v = np.moveaxis(np.asarray(x, np.float32).astype(ml_dtypes.bfloat16).astype(np.float64), axis, -1)
    blocks = v.reshape(v.shape[:-1] + (-1, 32))
    amax = np.abs(blocks).max(-1, keepdims=True)
    byte = np.maximum(np.where(amax > 0, np.frexp(amax)[1] - 1 + 127, 0) - down, 1)
    scale = np.exp2(byte - 127.0)
    codes = (blocks / scale).astype(np.float32).astype(dtype).astype(np.float64)
    return np.moveaxis((codes * scale).reshape(v.shape), -1, axis)


WIDE = False


def mx_kscale(k):
    if not WIDE:
        return np.ones(k)
    levels = np.array([10, -10, 5, -5, 0])
    a = np.random.permutation(np.resize(levels, k // 512 * 4)).reshape(k // 512, 4)
    idx = np.arange(k)
    return np.exp2(a[idx // 512, idx % 128 // 32])


BF16 = ml_dtypes.bfloat16


def bf(x):
    return np.asarray(x, np.float32).astype(BF16)


def f64(x):
    return np.asarray(x).astype(np.float64)


E2M1 = np.array([0.0, 0.5, 1.0, 1.5, 2.0, 3.0, 4.0, 6.0, -0.0, -0.5, -1.0, -1.5, -2.0, -3.0, -4.0, -6.0])


def pack_weight(w, fmt):
    k, n = w.shape
    w = f64(bf(w)).reshape(k // 32, 32, n)
    amax = np.abs(w).max(1)
    if fmt == "e4m3":
        byte = np.frexp(amax)[1] - 1 + 127 - 7
    else:
        mant, ex = np.frexp(amax / 6.0)
        byte = np.where(mant > 0.5, ex, ex - 1) + 127
    byte = np.clip(np.where(amax > 0, byte, 1), 1, 254)
    scaled = (w * np.exp2(127.0 - byte)[:, None, :]).reshape(k, n).astype(np.float32)
    by_word = np.ascontiguousarray(scaled.reshape(k // 512, 128, 4, n).transpose(0, 1, 3, 2))
    if fmt == "e4m3":
        words = by_word.astype(ml_dtypes.float8_e4m3fn).view(np.uint8)
    else:
        c = by_word.astype(ml_dtypes.float4_e2m1fn).view(np.uint8) & 0xF
        words = c[..., 0::2] | (c[..., 1::2] << 4)
    return np.ascontiguousarray(words), np.ascontiguousarray(byte.astype(np.uint8).reshape(k // 512, 16, n))


def unpack_weight(words, scales, fmt):
    g, p, n, _ = words.shape
    if fmt == "e4m3":
        vals = np.ascontiguousarray(words).view(ml_dtypes.float8_e4m3fn).astype(np.float64)
    else:
        nib = np.empty((g, p, n, 4), np.uint8)
        nib[..., 0::2] = words & 0xF
        nib[..., 1::2] = words >> 4
        vals = E2M1[nib]
    vals = vals * np.repeat(np.exp2(scales.astype(np.float64) - 127.0), 8, axis=1)[..., None]
    return vals.transpose(0, 1, 3, 2).reshape(g * 512, n)


B, U, I = 128, 2048, 1024
K = U + I
FMT = "e4m3"


def sigmoid(v):
    return 1.0 / (1.0 + np.exp(-v))


def setup_inputs():
    s = mx_kscale(K)
    inputs = bf(np.random.standard_normal((B, I)) * s[U:])
    h_tm1 = bf(np.random.standard_normal((B, U)) * s[:U])
    c_tm1 = bf(np.random.standard_normal((B, U)))
    words, scales = pack_weight(np.random.standard_normal((K, 4 * U)) / np.sqrt(K) / s[:, None], FMT)
    return {"inputs": inputs,
            "h_tm1": h_tm1,
            "c_tm1": c_tm1,
            "kernel_words": words,
            "kernel_scales": scales}


def reference(inputs, h_tm1, c_tm1, kernel_words, kernel_scales):
    a = np.concatenate([f64(h_tm1), f64(inputs)], axis=-1)
    z = mxq(a, 1, "e4m3") @ unpack_weight(kernel_words, kernel_scales, FMT)
    z0, z1, z2, z3 = np.split(z, 4, axis=-1)
    i = sigmoid(z0)
    f = sigmoid(z1)
    c_tilde = np.tanh(z2)
    o = sigmoid(z3)
    c = f * f64(c_tm1) + i * c_tilde
    h = o * np.tanh(c)
    return (h, c)

@@ -1,0 +1,138 @@
+from contextlib import ExitStack
+
+import concourse.mybir as mybir
+from concourse.masks import make_identity
+
+F32 = mybir.dt.float32
+BF16 = mybir.dt.bfloat16
+I32 = mybir.dt.int32
+U32 = mybir.dt.uint32
+U8 = mybir.dt.uint8
+FP8X4 = mybir.dt.float8_e4m3fn_x4
+ACT = mybir.ActivationFunctionType
+
+P = 128
+B, U, I = 128, 2048, 1024
+K = U + I
+PASSES = K // 512
+GATES = 4
+NT = 512
+CHUNKS = U // NT
+NBUF = 16
+
+FLOPS = 2 * B * K * GATES * U
+
+
+def tile_customlstmcell_w_kernel(tc, inputs, h_tm1, c_tm1, kernel_words, kernel_scales, out_0, out_1):
+    nc = tc.nc
+    with ExitStack() as ctx:
+        keep = ctx.enter_context(tc.tile_pool(name="keep", bufs=1))
+        wpool = ctx.enter_context(tc.tile_pool(name="weights", bufs=NBUF))
+        tailpool = ctx.enter_context(tc.tile_pool(name="tail", bufs=CHUNKS))
+        temp = ctx.enter_context(tc.tile_pool(name="temp", bufs=3))
+        psum = ctx.enter_context(tc.psum_pool(name="psum", bufs=8))
+
+        a_sb = keep.tile([P, K], BF16, name="a_sb", align_bytes=64)
+        nc.sync.dma_start(out=a_sb[:, 0:U], in_=h_tm1)
+        nc.sync.dma_start(out=a_sb[:, U:K], in_=inputs)
+        c_old = keep.tile([P, U], BF16, name="c_old")
+        nc.scalar.dma_start(out=c_old[:], in_=c_tm1)
+
+        planes_a = keep.tile([P, GATES * U], U8, name="planes_a", align_bytes=64)
+        planes_b = keep.tile([P, 2, U], U8, name="planes_b", align_bytes=64)
+        nc.vector.memset(planes_a[:].bitcast(I32), 0)
+        nc.vector.memset(planes_b[:].rearrange("p g n -> p (g n)").bitcast(I32), 0)
+        for q in range(4):
+            nc.sync.dma_start(
+                out=planes_a[32 * q : 32 * q + 16, :].bitcast(I32),
+                in_=kernel_scales[0:4, 4 * q : 4 * q + 4, :].bitcast(I32),
+            )
+        for g in range(4, PASSES):
+            for q in range(4):
+                nc.sync.dma_start(
+                    out=planes_b[32 * q : 32 * q + 16, g - 4, :].bitcast(I32),
+                    in_=kernel_scales[g, 4 * q : 4 * q + 4, :].rearrange("r (j n) -> j r n", j=GATES).bitcast(I32),
+                )
+
+        ident = keep.tile([P, P], F32, name="ident")
+        make_identity(nc, ident[:])
+        a_words = a_sb[:].bitcast(F32)
+        grouped = keep.tile([P, PASSES * 512], BF16, name="grouped", align_bytes=64)
+        a_codes = keep.tile([P, PASSES * P], U32, name="a_codes", align_bytes=64)
+        a_scales = keep.tile([P, PASSES * P], U8, name="a_scales", align_bytes=64)
+        for pair in range(PASSES // 2):
+            xt = psum.tile([P, 4, P], F32, name="bank")
+            for gg in range(2):
+                g = 2 * pair + gg
+                for u in range(2):
+                    nc.tensor.transpose(xt[:, 2 * gg + u, :], a_words[:, 256 * g + u : 256 * (g + 1) : 2], ident[:])
+            nc.vector.tensor_copy(
+                out=grouped[:, 1024 * pair : 1024 * (pair + 1)].bitcast(F32).rearrange("p (g m u) -> p g m u", g=2, u=2),
+                in_=xt[:].rearrange("p (g u) m -> p g m u", u=2),
+            )
+        nc.vector.quantize_mx(out=a_codes[:, 0:512].bitcast(FP8X4), scales=a_scales[:, 0:512], in_=grouped[:, 0:2048])
+        nc.vector.quantize_mx(out=a_codes[:, 512:768].bitcast(FP8X4), scales=a_scales[:, 512:768], in_=grouped[:, 2048:3072])
+
+        def plane(g, j, c):
+            if g < 4:
+                return planes_a[4 * g : P, U * j + NT * c : U * j + NT * (c + 1)]
+            return planes_b[4 * j : P, g - 4, NT * c : NT * (c + 1)]
+
+        i_sb = keep.tile([P, U], F32, name="i_sb")
+        fc_sb = keep.tile([P, U], F32, name="fc_sb")
+        c_sb = keep.tile([P, U], F32, name="c_sb")
+        tc_sb = keep.tile([P, U], F32, name="tc_sb")
+        h_sb = keep.tile([P, U], F32, name="h_sb")
+
+        for j in range(GATES):
+            z = []
+            for c in range(CHUNKS):
+                bank = psum.tile([P, NT], F32, name="bank")
+                z.append(bank)
+            for g in range(PASSES):
+                src = kernel_words[g].rearrange("p n t -> p (n t)")
+                last = j == GATES - 1 and g == PASSES - 1
+                rhs = []
+                if last:
+                    for c in range(CHUNKS):
+                        wt = tailpool.tile([P, NT], U32, name="wt", align_bytes=64)
+                        lo = 4 * (U * j + NT * c)
+                        nc.sync.dma_start(out=wt[:].bitcast(I32), in_=src[:, lo : lo + 4 * NT].bitcast(I32))
+                        rhs.append(wt[:])
+                else:
+                    w = wpool.tile([P, U], U32, name="w", align_bytes=64)
+                    nc.sync.dma_start(out=w[:].bitcast(I32), in_=src[:, 4 * U * j : 4 * U * (j + 1)].bitcast(I32))
+                    for c in range(CHUNKS):
+                        rhs.append(w[:, NT * c : NT * (c + 1)])
+                for c in range(CHUNKS):
+                    nc.tensor.matmul_mx(
+                        out=z[c][:],
+                        lhsT=a_codes[:, P * g : P * (g + 1)].bitcast(FP8X4),
+                        lhsT_scale=a_scales[:, P * g : P * (g + 1)],
+                        rhs=rhs[c].bitcast(FP8X4),
+                        rhs_scale=plane(g, j, c),
+                        start=(g == 0),
+                        stop=(g == PASSES - 1),
+                    )
+            for c in range(CHUNKS):
+                cols = slice(NT * c, NT * (c + 1))
+                if j == 0:
+                    nc.scalar.activation(out=i_sb[:, cols], in_=z[c][:], func=ACT.Sigmoid)
+                elif j == 1:
+                    f = temp.tile([P, NT], F32, name="f")
+                    nc.scalar.activation(out=f[:], in_=z[c][:], func=ACT.Sigmoid)
+                    nc.vector.tensor_mul(out=fc_sb[:, cols], in0=f[:], in1=c_old[:, cols])
+                elif j == 2:
+                    ct = temp.tile([P, NT], F32, name="ct")
+                    nc.scalar.activation(out=ct[:], in_=z[c][:], func=ACT.Tanh)
+                    nc.vector.tensor_mul(out=ct[:], in0=ct[:], in1=i_sb[:, cols])
+                    nc.vector.tensor_add(out=c_sb[:, cols], in0=ct[:], in1=fc_sb[:, cols])
+                    nc.scalar.activation(out=tc_sb[:, cols], in_=c_sb[:, cols], func=ACT.Tanh)
+                    if c % 2 == 1:
+                        half = slice(NT * (c - 1), NT * (c + 1))
+                        nc.scalar.dma_start(out=out_1[:, half], in_=c_sb[:, half])
+                else:
+                    o = temp.tile([P, NT], F32, name="o")
+                    nc.scalar.activation(out=o[:], in_=z[c][:], func=ACT.Sigmoid)
+                    nc.vector.tensor_mul(out=h_sb[:, cols], in0=o[:], in1=tc_sb[:, cols])
+                    nc.sync.dma_start(out=out_0[:, cols], in_=h_sb[:, cols])

@@ -38,24 +38,24 @@ def tile_customlstmcell_w_kernel(tc, inputs, h_tm1, c_tm1, kernel_words, kernel_
         c_old = keep.tile([P, U], BF16, name="c_old")
         nc.scalar.dma_start(out=c_old[:], in_=c_tm1)
 
-        planes_a = keep.tile([P, GATES * U], U8, name="planes_a", align_bytes=64)
-        planes_b = keep.tile([P, 2, U], U8, name="planes_b", align_bytes=64)
-        nc.vector.memset(planes_a[:].bitcast(I32), 0)
-        nc.vector.memset(planes_b[:].rearrange("p g n -> p (g n)").bitcast(I32), 0)
-        for q in range(4):
-            nc.sync.dma_start(
-                out=planes_a[32 * q : 32 * q + 16, :].bitcast(I32),
-                in_=kernel_scales[0:4, 4 * q : 4 * q + 4, :].bitcast(I32),
-            )
-        for g in range(4, PASSES):
-            for q in range(4):
-                nc.sync.dma_start(
-                    out=planes_b[32 * q : 32 * q + 16, g - 4, :].bitcast(I32),
-                    in_=kernel_scales[g, 4 * q : 4 * q + 4, :].rearrange("r (j n) -> j r n", j=GATES).bitcast(I32),
-                )
-
         ident = keep.tile([P, P], F32, name="ident")
         make_identity(nc, ident[:])
+
+        planes_a = keep.tile([P, GATES * U], U8, name="planes_a", align_bytes=64)
+        planes_b = keep.tile([P, GATES * U], U8, name="planes_b", align_bytes=64)
+        nc.vector.memset(planes_a[:].bitcast(I32), 0)
+        nc.vector.memset(planes_b[:].bitcast(I32), 0)
+        for q in range(4):
+            nc.gpsimd.dma_start(
+                out=planes_a[32 * q : 32 * q + 16, :].bitcast(F32),
+                in_=kernel_scales[0:4, 4 * q : 4 * q + 4, :].bitcast(F32),
+            )
+        for q in range(4):
+            nc.gpsimd.dma_start(
+                out=planes_b[32 * q : 32 * q + 8, :].bitcast(F32),
+                in_=kernel_scales[4:6, 4 * q : 4 * q + 4, :].bitcast(F32),
+            )
+
         a_words = a_sb[:].bitcast(F32)
         grouped = keep.tile([P, PASSES * 512], BF16, name="grouped", align_bytes=64)
         a_codes = keep.tile([P, PASSES * P], U32, name="a_codes", align_bytes=64)
@@ -76,7 +76,7 @@ def tile_customlstmcell_w_kernel(tc, inputs, h_tm1, c_tm1, kernel_words, kernel_
         def plane(g, j, c):
             if g < 4:
                 return planes_a[4 * g : P, U * j + NT * c : U * j + NT * (c + 1)]
-            return planes_b[4 * j : P, g - 4, NT * c : NT * (c + 1)]
+            return planes_b[4 * (g - 4) : P, U * j + NT * c : U * j + NT * (c + 1)]
 
         i_sb = keep.tile([P, U], F32, name="i_sb")
         fc_sb = keep.tile([P, U], F32, name="fc_sb")

@@ -31,6 +31,7 @@ def tile_customlstmcell_w_kernel(tc, inputs, h_tm1, c_tm1, kernel_words, kernel_
         tailpool = ctx.enter_context(tc.tile_pool(name="tail", bufs=CHUNKS))
         temp = ctx.enter_context(tc.tile_pool(name="temp", bufs=3))
         psum = ctx.enter_context(tc.psum_pool(name="psum", bufs=8))
+        ctx.enter_context(tc.manual_schedule())
 
         a_sb = keep.tile([P, K], BF16, name="a_sb", align_bytes=64)
         nc.sync.dma_start(out=a_sb[:, 0:U], in_=h_tm1)
@@ -38,24 +39,24 @@ def tile_customlstmcell_w_kernel(tc, inputs, h_tm1, c_tm1, kernel_words, kernel_
         c_old = keep.tile([P, U], BF16, name="c_old")
         nc.scalar.dma_start(out=c_old[:], in_=c_tm1)
 
+        planes_a = keep.tile([P, GATES * U], U8, name="planes_a", align_bytes=64)
+        planes_b = keep.tile([P, 2, U], U8, name="planes_b", align_bytes=64)
+        nc.vector.memset(planes_a[:].bitcast(I32), 0)
+        nc.vector.memset(planes_b[:].rearrange("p g n -> p (g n)").bitcast(I32), 0)
+        for q in range(4):
+            nc.sync.dma_start(
+                out=planes_a[32 * q : 32 * q + 16, :].bitcast(I32),
+                in_=kernel_scales[0:4, 4 * q : 4 * q + 4, :].bitcast(I32),
+            )
+        for g in range(4, PASSES):
+            for q in range(4):
+                nc.sync.dma_start(
+                    out=planes_b[32 * q : 32 * q + 16, g - 4, :].bitcast(I32),
+                    in_=kernel_scales[g, 4 * q : 4 * q + 4, :].rearrange("r (j n) -> j r n", j=GATES).bitcast(I32),
+                )
+
         ident = keep.tile([P, P], F32, name="ident")
         make_identity(nc, ident[:])
-
-        planes_a = keep.tile([P, GATES * U], U8, name="planes_a", align_bytes=64)
-        planes_b = keep.tile([P, GATES * U], U8, name="planes_b", align_bytes=64)
-        nc.vector.memset(planes_a[:].bitcast(I32), 0)
-        nc.vector.memset(planes_b[:].bitcast(I32), 0)
-        for q in range(4):
-            nc.gpsimd.dma_start(
-                out=planes_a[32 * q : 32 * q + 16, :].bitcast(F32),
-                in_=kernel_scales[0:4, 4 * q : 4 * q + 4, :].bitcast(F32),
-            )
-        for q in range(4):
-            nc.gpsimd.dma_start(
-                out=planes_b[32 * q : 32 * q + 8, :].bitcast(F32),
-                in_=kernel_scales[4:6, 4 * q : 4 * q + 4, :].bitcast(F32),
-            )
-
         a_words = a_sb[:].bitcast(F32)
         grouped = keep.tile([P, PASSES * 512], BF16, name="grouped", align_bytes=64)
         a_codes = keep.tile([P, PASSES * P], U32, name="a_codes", align_bytes=64)
@@ -76,7 +77,7 @@ def tile_customlstmcell_w_kernel(tc, inputs, h_tm1, c_tm1, kernel_words, kernel_
         def plane(g, j, c):
             if g < 4:
                 return planes_a[4 * g : P, U * j + NT * c : U * j + NT * (c + 1)]
-            return planes_b[4 * (g - 4) : P, U * j + NT * c : U * j + NT * (c + 1)]
+            return planes_b[4 * j : P, g - 4, NT * c : NT * (c + 1)]
 
         i_sb = keep.tile([P, U], F32, name="i_sb")
         fc_sb = keep.tile([P, U], F32, name="fc_sb")

@@ -115,6 +115,8 @@ def tile_customlstmcell_w_kernel(tc, inputs, h_tm1, c_tm1, kernel_words, kernel_
                         start=(g == 0),
                         stop=(g == PASSES - 1),
                     )
+            if j == GATES - 1:
+                nc.sync.dma_start(out=out_1, in_=c_sb[:])
             for c in range(CHUNKS):
                 cols = slice(NT * c, NT * (c + 1))
                 if j == 0:
@@ -129,9 +131,6 @@ def tile_customlstmcell_w_kernel(tc, inputs, h_tm1, c_tm1, kernel_words, kernel_
                     nc.vector.tensor_mul(out=ct[:], in0=ct[:], in1=i_sb[:, cols])
                     nc.vector.tensor_add(out=c_sb[:, cols], in0=ct[:], in1=fc_sb[:, cols])
                     nc.scalar.activation(out=tc_sb[:, cols], in_=c_sb[:, cols], func=ACT.Tanh)
-                    if c % 2 == 1:
-                        half = slice(NT * (c - 1), NT * (c + 1))
-                        nc.scalar.dma_start(out=out_1[:, half], in_=c_sb[:, half])
                 else:
                     o = temp.tile([P, NT], F32, name="o")
                     nc.scalar.activation(out=o[:], in_=z[c][:], func=ACT.Sigmoid)

@@ -18,7 +18,8 @@ PASSES = K // 512
 GATES = 4
 NT = 512
 CHUNKS = U // NT
-NBUF = 16
+PAIR_BUFS = 5
+SINGLE_BUFS = 6
 
 FLOPS = 2 * B * K * GATES * U
 
@@ -27,7 +28,8 @@ def tile_customlstmcell_w_kernel(tc, inputs, h_tm1, c_tm1, kernel_words, kernel_
     nc = tc.nc
     with ExitStack() as ctx:
         keep = ctx.enter_context(tc.tile_pool(name="keep", bufs=1))
-        wpool = ctx.enter_context(tc.tile_pool(name="weights", bufs=NBUF))
+        pairpool = ctx.enter_context(tc.tile_pool(name="pairs", bufs=PAIR_BUFS))
+        wpool = ctx.enter_context(tc.tile_pool(name="weights", bufs=SINGLE_BUFS))
         tailpool = ctx.enter_context(tc.tile_pool(name="tail", bufs=CHUNKS))
         temp = ctx.enter_context(tc.tile_pool(name="temp", bufs=3))
         psum = ctx.enter_context(tc.psum_pool(name="psum", bufs=8))
@@ -85,54 +87,73 @@ def tile_customlstmcell_w_kernel(tc, inputs, h_tm1, c_tm1, kernel_words, kernel_
         tc_sb = keep.tile([P, U], F32, name="tc_sb")
         h_sb = keep.tile([P, U], F32, name="h_sb")
 
-        for j in range(GATES):
-            z = []
-            for c in range(CHUNKS):
-                bank = psum.tile([P, NT], F32, name="bank")
-                z.append(bank)
+        units = []
+        for g in range(PASSES):
+            units.append(((0, 1), g))
+        for j in (2, 3):
             for g in range(PASSES):
-                src = kernel_words[g].rearrange("p n t -> p (n t)")
-                last = j == GATES - 1 and g == PASSES - 1
-                rhs = []
-                if last:
-                    for c in range(CHUNKS):
-                        wt = tailpool.tile([P, NT], U32, name="wt", align_bytes=64)
-                        lo = 4 * (U * j + NT * c)
-                        nc.sync.dma_start(out=wt[:].bitcast(I32), in_=src[:, lo : lo + 4 * NT].bitcast(I32))
-                        rhs.append(wt[:])
-                else:
-                    w = wpool.tile([P, U], U32, name="w", align_bytes=64)
-                    nc.sync.dma_start(out=w[:].bitcast(I32), in_=src[:, 4 * U * j : 4 * U * (j + 1)].bitcast(I32))
-                    for c in range(CHUNKS):
-                        rhs.append(w[:, NT * c : NT * (c + 1)])
+                units.append(((j,), g))
+
+        z = {}
+        for n, (gates, g) in enumerate(units):
+            src = kernel_words[g].rearrange("p n t -> p (n t)")
+            first_col = U * gates[0]
+            width = U * len(gates)
+            rhs = {}
+            if n == len(units) - 1:
                 for c in range(CHUNKS):
+                    wt = tailpool.tile([P, NT], U32, name="wt", align_bytes=64)
+                    lo = 4 * (first_col + NT * c)
+                    nc.sync.dma_start(out=wt[:].bitcast(I32), in_=src[:, lo : lo + 4 * NT].bitcast(I32))
+                    rhs[(gates[0], c)] = wt[:]
+            else:
+                if len(gates) == 2:
+                    w = pairpool.tile([P, width], U32, name="w2", align_bytes=64)
+                else:
+                    w = wpool.tile([P, width], U32, name="w", align_bytes=64)
+                nc.sync.dma_start(out=w[:].bitcast(I32), in_=src[:, 4 * first_col : 4 * (first_col + width)].bitcast(I32))
+                for k, j in enumerate(gates):
+                    for c in range(CHUNKS):
+                        rhs[(j, c)] = w[:, U * k + NT * c : U * k + NT * (c + 1)]
+            for j in gates:
+                for c in range(CHUNKS):
+                    if g == 0:
+                        bank = psum.tile([P, NT], F32, name="bank")
+                        z[(j, c)] = bank
                     nc.tensor.matmul_mx(
-                        out=z[c][:],
+                        out=z[(j, c)][:],
                         lhsT=a_codes[:, P * g : P * (g + 1)].bitcast(FP8X4),
                         lhsT_scale=a_scales[:, P * g : P * (g + 1)],
-                        rhs=rhs[c].bitcast(FP8X4),
+                        rhs=rhs[(j, c)].bitcast(FP8X4),
                         rhs_scale=plane(g, j, c),
                         start=(g == 0),
                         stop=(g == PASSES - 1),
                     )
-            if j == GATES - 1:
+            if g < PASSES - 1:
+                continue
+            if n == len(units) - 1:
                 nc.sync.dma_start(out=out_1, in_=c_sb[:])
-            for c in range(CHUNKS):
-                cols = slice(NT * c, NT * (c + 1))
-                if j == 0:
-                    nc.scalar.activation(out=i_sb[:, cols], in_=z[c][:], func=ACT.Sigmoid)
-                elif j == 1:
-                    f = temp.tile([P, NT], F32, name="f")
-                    nc.scalar.activation(out=f[:], in_=z[c][:], func=ACT.Sigmoid)
-                    nc.vector.tensor_mul(out=fc_sb[:, cols], in0=f[:], in1=c_old[:, cols])
-                elif j == 2:
-                    ct = temp.tile([P, NT], F32, name="ct")
-                    nc.scalar.activation(out=ct[:], in_=z[c][:], func=ACT.Tanh)
-                    nc.vector.tensor_mul(out=ct[:], in0=ct[:], in1=i_sb[:, cols])
-                    nc.vector.tensor_add(out=c_sb[:, cols], in0=ct[:], in1=fc_sb[:, cols])
-                    nc.scalar.activation(out=tc_sb[:, cols], in_=c_sb[:, cols], func=ACT.Tanh)
-                else:
-                    o = temp.tile([P, NT], F32, name="o")
-                    nc.scalar.activation(out=o[:], in_=z[c][:], func=ACT.Sigmoid)
-                    nc.vector.tensor_mul(out=h_sb[:, cols], in0=o[:], in1=tc_sb[:, cols])
-                    nc.sync.dma_start(out=out_0[:, cols], in_=h_sb[:, cols])
+            for j in gates:
+                for c in range(CHUNKS):
+                    cols = slice(NT * c, NT * (c + 1))
+                    acc = z[(j, c)]
+                    if j == 0:
+                        nc.scalar.activation(out=i_sb[:, cols], in_=acc[:], func=ACT.Sigmoid)
+                    elif j == 1:
+                        f = temp.tile([P, NT], F32, name="f")
+                        nc.scalar.activation(out=f[:], in_=acc[:], func=ACT.Sigmoid)
+                        nc.vector.tensor_mul(out=fc_sb[:, cols], in0=f[:], in1=c_old[:, cols])
+                    elif j == 2:
+                        ct = temp.tile([P, NT], F32, name="ct")
+                        nc.scalar.activation(out=ct[:], in_=acc[:], func=ACT.Tanh)
+                        nc.vector.tensor_mul(out=ct[:], in0=ct[:], in1=i_sb[:, cols])
+                        nc.vector.tensor_add(out=c_sb[:, cols], in0=ct[:], in1=fc_sb[:, cols])
+                    else:
+                        o = temp.tile([P, NT], F32, name="o")
+                        nc.scalar.activation(out=o[:], in_=acc[:], func=ACT.Sigmoid)
+                        nc.vector.tensor_mul(out=h_sb[:, cols], in0=o[:], in1=tc_sb[:, cols])
+                        nc.sync.dma_start(out=out_0[:, cols], in_=h_sb[:, cols])
+                if j == 2:
+                    for c in range(CHUNKS):
+                        cols = slice(NT * c, NT * (c + 1))
+                        nc.scalar.activation(out=tc_sb[:, cols], in_=c_sb[:, cols], func=ACT.Tanh)

@@ -18,8 +18,7 @@ PASSES = K // 512
 GATES = 4
 NT = 512
 CHUNKS = U // NT
-PAIR_BUFS = 5
-SINGLE_BUFS = 6
+NBUF = 16
 
 FLOPS = 2 * B * K * GATES * U
 
@@ -28,8 +27,7 @@ def tile_customlstmcell_w_kernel(tc, inputs, h_tm1, c_tm1, kernel_words, kernel_
     nc = tc.nc
     with ExitStack() as ctx:
         keep = ctx.enter_context(tc.tile_pool(name="keep", bufs=1))
-        pairpool = ctx.enter_context(tc.tile_pool(name="pairs", bufs=PAIR_BUFS))
-        wpool = ctx.enter_context(tc.tile_pool(name="weights", bufs=SINGLE_BUFS))
+        wpool = ctx.enter_context(tc.tile_pool(name="weights", bufs=NBUF))
         tailpool = ctx.enter_context(tc.tile_pool(name="tail", bufs=CHUNKS))
         temp = ctx.enter_context(tc.tile_pool(name="temp", bufs=3))
         psum = ctx.enter_context(tc.psum_pool(name="psum", bufs=8))
@@ -41,24 +39,30 @@ def tile_customlstmcell_w_kernel(tc, inputs, h_tm1, c_tm1, kernel_words, kernel_
         c_old = keep.tile([P, U], BF16, name="c_old")
         nc.scalar.dma_start(out=c_old[:], in_=c_tm1)
 
+        ident = keep.tile([P, P], F32, name="ident")
+        make_identity(nc, ident[:])
+
         planes_a = keep.tile([P, GATES * U], U8, name="planes_a", align_bytes=64)
         planes_b = keep.tile([P, 2, U], U8, name="planes_b", align_bytes=64)
         nc.vector.memset(planes_a[:].bitcast(I32), 0)
         nc.vector.memset(planes_b[:].rearrange("p g n -> p (g n)").bitcast(I32), 0)
-        for q in range(4):
+        for q in range(2):
             nc.sync.dma_start(
                 out=planes_a[32 * q : 32 * q + 16, :].bitcast(I32),
                 in_=kernel_scales[0:4, 4 * q : 4 * q + 4, :].bitcast(I32),
             )
-        for g in range(4, PASSES):
-            for q in range(4):
+        for q in range(2, 4):
+            nc.gpsimd.dma_start(
+                out=planes_a[32 * q : 32 * q + 16, :].bitcast(F32),
+                in_=kernel_scales[0:4, 4 * q : 4 * q + 4, :].bitcast(F32),
+            )
+        for q in range(4):
+            for g in range(4, PASSES):
                 nc.sync.dma_start(
                     out=planes_b[32 * q : 32 * q + 16, g - 4, :].bitcast(I32),
                     in_=kernel_scales[g, 4 * q : 4 * q + 4, :].rearrange("r (j n) -> j r n", j=GATES).bitcast(I32),
                 )
 
-        ident = keep.tile([P, P], F32, name="ident")
-        make_identity(nc, ident[:])
         a_words = a_sb[:].bitcast(F32)
         grouped = keep.tile([P, PASSES * 512], BF16, name="grouped", align_bytes=64)
         a_codes = keep.tile([P, PASSES * P], U32, name="a_codes", align_bytes=64)
@@ -87,73 +91,54 @@ def tile_customlstmcell_w_kernel(tc, inputs, h_tm1, c_tm1, kernel_words, kernel_
         tc_sb = keep.tile([P, U], F32, name="tc_sb")
         h_sb = keep.tile([P, U], F32, name="h_sb")
 
-        units = []
-        for g in range(PASSES):
-            units.append(((0, 1), g))
-        for j in (2, 3):
+        for j in range(GATES):
+            z = []
+            for c in range(CHUNKS):
+                bank = psum.tile([P, NT], F32, name="bank")
+                z.append(bank)
             for g in range(PASSES):
-                units.append(((j,), g))
-
-        z = {}
-        for n, (gates, g) in enumerate(units):
-            src = kernel_words[g].rearrange("p n t -> p (n t)")
-            first_col = U * gates[0]
-            width = U * len(gates)
-            rhs = {}
-            if n == len(units) - 1:
-                for c in range(CHUNKS):
-                    wt = tailpool.tile([P, NT], U32, name="wt", align_bytes=64)
-                    lo = 4 * (first_col + NT * c)
-                    nc.sync.dma_start(out=wt[:].bitcast(I32), in_=src[:, lo : lo + 4 * NT].bitcast(I32))
-                    rhs[(gates[0], c)] = wt[:]
-            else:
-                if len(gates) == 2:
-                    w = pairpool.tile([P, width], U32, name="w2", align_bytes=64)
-                else:
-                    w = wpool.tile([P, width], U32, name="w", align_bytes=64)
-                nc.sync.dma_start(out=w[:].bitcast(I32), in_=src[:, 4 * first_col : 4 * (first_col + width)].bitcast(I32))
-                for k, j in enumerate(gates):
+                src = kernel_words[g].rearrange("p n t -> p (n t)")
+                last = j == GATES - 1 and g == PASSES - 1
+                rhs = []
+                if last:
                     for c in range(CHUNKS):
-                        rhs[(j, c)] = w[:, U * k + NT * c : U * k + NT * (c + 1)]
-            for j in gates:
+                        wt = tailpool.tile([P, NT], U32, name="wt", align_bytes=64)
+                        lo = 4 * (U * j + NT * c)
+                        nc.sync.dma_start(out=wt[:].bitcast(I32), in_=src[:, lo : lo + 4 * NT].bitcast(I32))
+                        rhs.append(wt[:])
+                else:
+                    w = wpool.tile([P, U], U32, name="w", align_bytes=64)
+                    nc.sync.dma_start(out=w[:].bitcast(I32), in_=src[:, 4 * U * j : 4 * U * (j + 1)].bitcast(I32))
+                    for c in range(CHUNKS):
+                        rhs.append(w[:, NT * c : NT * (c + 1)])
                 for c in range(CHUNKS):
-                    if g == 0:
-                        bank = psum.tile([P, NT], F32, name="bank")
-                        z[(j, c)] = bank
                     nc.tensor.matmul_mx(
-                        out=z[(j, c)][:],
+                        out=z[c][:],
                         lhsT=a_codes[:, P * g : P * (g + 1)].bitcast(FP8X4),
                         lhsT_scale=a_scales[:, P * g : P * (g + 1)],
-                        rhs=rhs[(j, c)].bitcast(FP8X4),
+                        rhs=rhs[c].bitcast(FP8X4),
                         rhs_scale=plane(g, j, c),
                         start=(g == 0),
                         stop=(g == PASSES - 1),
                     )
-            if g < PASSES - 1:
-                continue
-            if n == len(units) - 1:
+            if j == GATES - 1:
                 nc.sync.dma_start(out=out_1, in_=c_sb[:])
-            for j in gates:
-                for c in range(CHUNKS):
-                    cols = slice(NT * c, NT * (c + 1))
-                    acc = z[(j, c)]
-                    if j == 0:
-                        nc.scalar.activation(out=i_sb[:, cols], in_=acc[:], func=ACT.Sigmoid)
-                    elif j == 1:
-                        f = temp.tile([P, NT], F32, name="f")
-                        nc.scalar.activation(out=f[:], in_=acc[:], func=ACT.Sigmoid)
-                        nc.vector.tensor_mul(out=fc_sb[:, cols], in0=f[:], in1=c_old[:, cols])
-                    elif j == 2:
-                        ct = temp.tile([P, NT], F32, name="ct")
-                        nc.scalar.activation(out=ct[:], in_=acc[:], func=ACT.Tanh)
-                        nc.vector.tensor_mul(out=ct[:], in0=ct[:], in1=i_sb[:, cols])
-                        nc.vector.tensor_add(out=c_sb[:, cols], in0=ct[:], in1=fc_sb[:, cols])
-                    else:
-                        o = temp.tile([P, NT], F32, name="o")
-                        nc.scalar.activation(out=o[:], in_=acc[:], func=ACT.Sigmoid)
-                        nc.vector.tensor_mul(out=h_sb[:, cols], in0=o[:], in1=tc_sb[:, cols])
-                        nc.sync.dma_start(out=out_0[:, cols], in_=h_sb[:, cols])
-                if j == 2:
-                    for c in range(CHUNKS):
-                        cols = slice(NT * c, NT * (c + 1))
-                        nc.scalar.activation(out=tc_sb[:, cols], in_=c_sb[:, cols], func=ACT.Tanh)
+            for c in range(CHUNKS):
+                cols = slice(NT * c, NT * (c + 1))
+                if j == 0:
+                    nc.scalar.activation(out=i_sb[:, cols], in_=z[c][:], func=ACT.Sigmoid)
+                elif j == 1:
+                    f = temp.tile([P, NT], F32, name="f")
+                    nc.scalar.activation(out=f[:], in_=z[c][:], func=ACT.Sigmoid)
+                    nc.vector.tensor_mul(out=fc_sb[:, cols], in0=f[:], in1=c_old[:, cols])
+                elif j == 2:
+                    ct = temp.tile([P, NT], F32, name="ct")
+                    nc.scalar.activation(out=ct[:], in_=z[c][:], func=ACT.Tanh)
+                    nc.vector.tensor_mul(out=ct[:], in0=ct[:], in1=i_sb[:, cols])
+                    nc.vector.tensor_add(out=c_sb[:, cols], in0=ct[:], in1=fc_sb[:, cols])
+                    nc.scalar.activation(out=tc_sb[:, cols], in_=c_sb[:, cols], func=ACT.Tanh)
+                else:
+                    o = temp.tile([P, NT], F32, name="o")
+                    nc.scalar.activation(out=o[:], in_=z[c][:], func=ACT.Sigmoid)
+                    nc.vector.tensor_mul(out=h_sb[:, cols], in0=o[:], in1=tc_sb[:, cols])
+                    nc.sync.dma_start(out=out_0[:, cols], in_=h_sb[:, cols])

@@ -44,24 +44,30 @@ def tile_customlstmcell_w_kernel(tc, inputs, h_tm1, c_tm1, kernel_words, kernel_
 
         planes_a = keep.tile([P, GATES * U], U8, name="planes_a", align_bytes=64)
         planes_b = keep.tile([P, 2, U], U8, name="planes_b", align_bytes=64)
-        nc.vector.memset(planes_a[:].bitcast(I32), 0)
         nc.vector.memset(planes_b[:].rearrange("p g n -> p (g n)").bitcast(I32), 0)
-        for q in range(2):
-            nc.sync.dma_start(
-                out=planes_a[32 * q : 32 * q + 16, :].bitcast(I32),
-                in_=kernel_scales[0:4, 4 * q : 4 * q + 4, :].bitcast(I32),
+        nc.vector.memset(planes_a[:].bitcast(I32), 0)
+
+        def load_a(queue, view, q):
+            queue.dma_start(
+                out=planes_a[32 * q : 32 * q + 16, :].bitcast(view),
+                in_=kernel_scales[0:4, 4 * q : 4 * q + 4, :].bitcast(view),
             )
-        for q in range(2, 4):
-            nc.gpsimd.dma_start(
-                out=planes_a[32 * q : 32 * q + 16, :].bitcast(F32),
-                in_=kernel_scales[0:4, 4 * q : 4 * q + 4, :].bitcast(F32),
+
+        def load_b(queue, view, g, q):
+            queue.dma_start(
+                out=planes_b[32 * q : 32 * q + 16, g - 4, :].bitcast(view),
+                in_=kernel_scales[g, 4 * q : 4 * q + 4, :].rearrange("r (j n) -> j r n", j=GATES).bitcast(view),
             )
-        for q in range(4):
-            for g in range(4, PASSES):
-                nc.sync.dma_start(
-                    out=planes_b[32 * q : 32 * q + 16, g - 4, :].bitcast(I32),
-                    in_=kernel_scales[g, 4 * q : 4 * q + 4, :].rearrange("r (j n) -> j r n", j=GATES).bitcast(I32),
-                )
+
+        load_b(nc.gpsimd, F32, 4, 2)
+        load_a(nc.gpsimd, F32, 2)
+        load_a(nc.gpsimd, F32, 3)
+        load_b(nc.gpsimd, F32, 5, 2)
+        load_a(nc.sync, I32, 0)
+        load_a(nc.sync, I32, 1)
+        for q in (0, 1, 3):
+            for g in (4, 5):
+                load_b(nc.sync, I32, g, q)
 
         a_words = a_sb[:].bitcast(F32)
         grouped = keep.tile([P, PASSES * 512], BF16, name="grouped", align_bytes=64)

@@ -29,7 +29,7 @@ def tile_customlstmcell_w_kernel(tc, inputs, h_tm1, c_tm1, kernel_words, kernel_
         keep = ctx.enter_context(tc.tile_pool(name="keep", bufs=1))
         wpool = ctx.enter_context(tc.tile_pool(name="weights", bufs=NBUF))
         tailpool = ctx.enter_context(tc.tile_pool(name="tail", bufs=CHUNKS))
-        temp = ctx.enter_context(tc.tile_pool(name="temp", bufs=3))
+        temp = ctx.enter_context(tc.tile_pool(name="temp", bufs=4))
         psum = ctx.enter_context(tc.psum_pool(name="psum", bufs=8))
         ctx.enter_context(tc.manual_schedule())
 
@@ -59,15 +59,18 @@ def tile_customlstmcell_w_kernel(tc, inputs, h_tm1, c_tm1, kernel_words, kernel_
                 in_=kernel_scales[g, 4 * q : 4 * q + 4, :].rearrange("r (j n) -> j r n", j=GATES).bitcast(view),
             )
 
+        load_b(nc.gpsimd, F32, 4, 0)
         load_b(nc.gpsimd, F32, 4, 2)
         load_a(nc.gpsimd, F32, 2)
-        load_a(nc.gpsimd, F32, 3)
         load_b(nc.gpsimd, F32, 5, 2)
+        load_b(nc.gpsimd, F32, 4, 1)
+        load_b(nc.gpsimd, F32, 4, 3)
+        load_a(nc.gpsimd, F32, 3)
+        load_b(nc.gpsimd, F32, 5, 3)
         load_a(nc.sync, I32, 0)
         load_a(nc.sync, I32, 1)
-        for q in (0, 1, 3):
-            for g in (4, 5):
-                load_b(nc.sync, I32, g, q)
+        load_b(nc.sync, I32, 5, 0)
+        load_b(nc.sync, I32, 5, 1)
 
         a_words = a_sb[:].bitcast(F32)
         grouped = keep.tile([P, PASSES * 512], BF16, name="grouped", align_bytes=64)
@@ -142,9 +145,12 @@ def tile_customlstmcell_w_kernel(tc, inputs, h_tm1, c_tm1, kernel_words, kernel_
                     nc.scalar.activation(out=ct[:], in_=z[c][:], func=ACT.Tanh)
                     nc.vector.tensor_mul(out=ct[:], in0=ct[:], in1=i_sb[:, cols])
                     nc.vector.tensor_add(out=c_sb[:, cols], in0=ct[:], in1=fc_sb[:, cols])
-                    nc.scalar.activation(out=tc_sb[:, cols], in_=c_sb[:, cols], func=ACT.Tanh)
                 else:
                     o = temp.tile([P, NT], F32, name="o")
                     nc.scalar.activation(out=o[:], in_=z[c][:], func=ACT.Sigmoid)
                     nc.vector.tensor_mul(out=h_sb[:, cols], in0=o[:], in1=tc_sb[:, cols])
                     nc.sync.dma_start(out=out_0[:, cols], in_=h_sb[:, cols])
+            if j == 2:
+                for c in range(CHUNKS):
+                    cols = slice(NT * c, NT * (c + 1))
+                    nc.scalar.activation(out=tc_sb[:, cols], in_=c_sb[:, cols], func=ACT.Tanh)

from contextlib import ExitStack

import concourse.mybir as mybir
from concourse.masks import make_identity

F32 = mybir.dt.float32
BF16 = mybir.dt.bfloat16
I32 = mybir.dt.int32
U32 = mybir.dt.uint32
U8 = mybir.dt.uint8
FP8X4 = mybir.dt.float8_e4m3fn_x4
ACT = mybir.ActivationFunctionType

P = 128
B, U, I = 128, 2048, 1024
K = U + I
PASSES = K // 512
GATES = 4
NT = 512
CHUNKS = U // NT
NBUF = 16

FLOPS = 2 * B * K * GATES * U


def tile_customlstmcell_w_kernel(tc, inputs, h_tm1, c_tm1, kernel_words, kernel_scales, out_0, out_1):
    nc = tc.nc
    with ExitStack() as ctx:
        keep = ctx.enter_context(tc.tile_pool(name="keep", bufs=1))
        wpool = ctx.enter_context(tc.tile_pool(name="weights", bufs=NBUF))
        tailpool = ctx.enter_context(tc.tile_pool(name="tail", bufs=CHUNKS))
        temp = ctx.enter_context(tc.tile_pool(name="temp", bufs=4))
        psum = ctx.enter_context(tc.psum_pool(name="psum", bufs=8))
        ctx.enter_context(tc.manual_schedule())

        a_sb = keep.tile([P, K], BF16, name="a_sb", align_bytes=64)
        nc.sync.dma_start(out=a_sb[:, 0:U], in_=h_tm1)
        nc.sync.dma_start(out=a_sb[:, U:K], in_=inputs)
        c_old = keep.tile([P, U], BF16, name="c_old")
        nc.scalar.dma_start(out=c_old[:], in_=c_tm1)

        ident = keep.tile([P, P], F32, name="ident")
        make_identity(nc, ident[:])

        planes_a = keep.tile([P, GATES * U], U8, name="planes_a", align_bytes=64)
        planes_b = keep.tile([P, 2, U], U8, name="planes_b", align_bytes=64)
        nc.vector.memset(planes_b[:].rearrange("p g n -> p (g n)").bitcast(I32), 0)
        nc.vector.memset(planes_a[:].bitcast(I32), 0)

        def load_a(queue, view, q):
            queue.dma_start(
                out=planes_a[32 * q : 32 * q + 16, :].bitcast(view),
                in_=kernel_scales[0:4, 4 * q : 4 * q + 4, :].bitcast(view),
            )

        def load_b(queue, view, g, q):
            queue.dma_start(
                out=planes_b[32 * q : 32 * q + 16, g - 4, :].bitcast(view),
                in_=kernel_scales[g, 4 * q : 4 * q + 4, :].rearrange("r (j n) -> j r n", j=GATES).bitcast(view),
            )

        load_b(nc.gpsimd, F32, 4, 0)
        load_b(nc.gpsimd, F32, 4, 2)
        load_a(nc.gpsimd, F32, 2)
        load_b(nc.gpsimd, F32, 5, 2)
        load_b(nc.gpsimd, F32, 4, 1)
        load_b(nc.gpsimd, F32, 4, 3)
        load_a(nc.gpsimd, F32, 3)
        load_b(nc.gpsimd, F32, 5, 3)
        load_a(nc.sync, I32, 0)
        load_a(nc.sync, I32, 1)
        load_b(nc.sync, I32, 5, 0)
        load_b(nc.sync, I32, 5, 1)

        a_words = a_sb[:].bitcast(F32)
        grouped = keep.tile([P, PASSES * 512], BF16, name="grouped", align_bytes=64)
        a_codes = keep.tile([P, PASSES * P], U32, name="a_codes", align_bytes=64)
        a_scales = keep.tile([P, PASSES * P], U8, name="a_scales", align_bytes=64)
        for pair in range(PASSES // 2):
            xt = psum.tile([P, 4, P], F32, name="bank")
            for gg in range(2):
                g = 2 * pair + gg
                for u in range(2):
                    nc.tensor.transpose(xt[:, 2 * gg + u, :], a_words[:, 256 * g + u : 256 * (g + 1) : 2], ident[:])
            nc.vector.tensor_copy(
                out=grouped[:, 1024 * pair : 1024 * (pair + 1)].bitcast(F32).rearrange("p (g m u) -> p g m u", g=2, u=2),
                in_=xt[:].rearrange("p (g u) m -> p g m u", u=2),
            )
        nc.vector.quantize_mx(out=a_codes[:, 0:512].bitcast(FP8X4), scales=a_scales[:, 0:512], in_=grouped[:, 0:2048])
        nc.vector.quantize_mx(out=a_codes[:, 512:768].bitcast(FP8X4), scales=a_scales[:, 512:768], in_=grouped[:, 2048:3072])

        def plane(g, j, c):
            if g < 4:
                return planes_a[4 * g : P, U * j + NT * c : U * j + NT * (c + 1)]
            return planes_b[4 * j : P, g - 4, NT * c : NT * (c + 1)]

        i_sb = keep.tile([P, U], F32, name="i_sb")
        fc_sb = keep.tile([P, U], F32, name="fc_sb")
        c_sb = keep.tile([P, U], F32, name="c_sb")
        tc_sb = keep.tile([P, U], F32, name="tc_sb")
        h_sb = keep.tile([P, U], F32, name="h_sb")

        for j in range(GATES):
            z = []
            for c in range(CHUNKS):
                bank = psum.tile([P, NT], F32, name="bank")
                z.append(bank)
            for g in range(PASSES):
                src = kernel_words[g].rearrange("p n t -> p (n t)")
                last = j == GATES - 1 and g == PASSES - 1
                rhs = []
                if last:
                    for c in range(CHUNKS):
                        wt = tailpool.tile([P, NT], U32, name="wt", align_bytes=64)
                        lo = 4 * (U * j + NT * c)
                        nc.sync.dma_start(out=wt[:].bitcast(I32), in_=src[:, lo : lo + 4 * NT].bitcast(I32))
                        rhs.append(wt[:])
                else:
                    w = wpool.tile([P, U], U32, name="w", align_bytes=64)
                    nc.sync.dma_start(out=w[:].bitcast(I32), in_=src[:, 4 * U * j : 4 * U * (j + 1)].bitcast(I32))
                    for c in range(CHUNKS):
                        rhs.append(w[:, NT * c : NT * (c + 1)])
                for c in range(CHUNKS):
                    nc.tensor.matmul_mx(
                        out=z[c][:],
                        lhsT=a_codes[:, P * g : P * (g + 1)].bitcast(FP8X4),
                        lhsT_scale=a_scales[:, P * g : P * (g + 1)],
                        rhs=rhs[c].bitcast(FP8X4),
                        rhs_scale=plane(g, j, c),
                        start=(g == 0),
                        stop=(g == PASSES - 1),
                    )
            if j == GATES - 1:
                nc.sync.dma_start(out=out_1, in_=c_sb[:])
            for c in range(CHUNKS):
                cols = slice(NT * c, NT * (c + 1))
                if j == 0:
                    nc.scalar.activation(out=i_sb[:, cols], in_=z[c][:], func=ACT.Sigmoid)
                elif j == 1:
                    f = temp.tile([P, NT], F32, name="f")
                    nc.scalar.activation(out=f[:], in_=z[c][:], func=ACT.Sigmoid)
                    nc.vector.tensor_mul(out=fc_sb[:, cols], in0=f[:], in1=c_old[:, cols])
                elif j == 2:
                    ct = temp.tile([P, NT], F32, name="ct")
                    nc.scalar.activation(out=ct[:], in_=z[c][:], func=ACT.Tanh)
                    nc.vector.tensor_mul(out=ct[:], in0=ct[:], in1=i_sb[:, cols])
                    nc.vector.tensor_add(out=c_sb[:, cols], in0=ct[:], in1=fc_sb[:, cols])
                else:
                    o = temp.tile([P, NT], F32, name="o")
                    nc.scalar.activation(out=o[:], in_=z[c][:], func=ACT.Sigmoid)
                    nc.vector.tensor_mul(out=h_sb[:, cols], in0=o[:], in1=tc_sb[:, cols])
                    nc.sync.dma_start(out=out_0[:, cols], in_=h_sb[:, cols])
            if j == 2:
                for c in range(CHUNKS):
                    cols = slice(NT * c, NT * (c + 1))
                    nc.scalar.activation(out=tc_sb[:, cols], in_=c_sb[:, cols], func=ACT.Tanh)
